import numpy as np
import ml_dtypes


def mxq(x, axis, fmt="e4m3"):
    dtype, down = {"e4m3": (ml_dtypes.float8_e4m3fn, 7), "e5m2": (ml_dtypes.float8_e5m2, 14)}[fmt]
    v = np.moveaxis(np.asarray(x, np.float32).astype(ml_dtypes.bfloat16).astype(np.float64), axis, -1)
    blocks = v.reshape(v.shape[:-1] + (-1, 32))
    amax = np.abs(blocks).max(-1, keepdims=True)
    byte = np.maximum(np.where(amax > 0, np.frexp(amax)[1] - 1 + 127, 0) - down, 1)
    scale = np.exp2(byte - 127.0)
    codes = (blocks / scale).astype(np.float32).astype(dtype).astype(np.float64)
    return np.moveaxis((codes * scale).reshape(v.shape), -1, axis)


WIDE = False


def mx_kscale(k):
    if not WIDE:
        return np.ones(k)
    levels = np.array([10, -10, 5, -5, 0])
    a = np.random.permutation(np.resize(levels, k // 512 * 4)).reshape(k // 512, 4)
    idx = np.arange(k)
    return np.exp2(a[idx // 512, idx % 128 // 32])


BF16 = ml_dtypes.bfloat16


def bf(x):
    return np.asarray(x, np.float32).astype(BF16)


def f64(x):
    return np.asarray(x).astype(np.float64)


B, S, DIM, HID, R, NT = 8, 512, 1024, 512, 128, 3
SCALING = 4.0


def silu(v):
    return v / (1.0 + np.exp(-v))


def lora_out(xa, bw, tw):
    return (xa @ bw) * SCALING * tw[..., None]


def setup_inputs():
    s = mx_kscale(DIM)
    return {"x": bf(np.random.standard_normal((B, S, DIM)) * s),
            "w1": bf(np.random.standard_normal((DIM, HID)) / np.sqrt(DIM) / s[:, None]),
            "w3": bf(np.random.standard_normal((DIM, HID)) / np.sqrt(DIM) / s[:, None]),
            "xa_up": bf(np.random.standard_normal((B, S, R))),
            "b_up": bf(np.random.standard_normal((R, HID)) * 0.2 / np.sqrt(R)),
            "xa_gate": bf(np.random.standard_normal((B, S, R))),
            "b_gate": bf(np.random.standard_normal((R, HID)) * 0.2 / np.sqrt(R)),
            "tw_up": bf(np.random.uniform(size=(B, S))),
            "tw_gate": bf(np.random.uniform(size=(B, S)))}


def reference(x, w1, w3, xa_up, b_up, xa_gate, b_gate, tw_up, tw_gate):
    xq = mxq(f64(x), 2, "e4m3")
    up = (xq @ mxq(f64(w3), 0, "e4m3")) + lora_out(f64(xa_up), f64(b_up), f64(tw_up))
    gate = silu((xq @ mxq(f64(w1), 0, "e4m3")) + lora_out(f64(xa_gate), f64(b_gate), f64(tw_gate)))
    return gate * up

@@ -1,0 +1,230 @@
+from contextlib import ExitStack
+
+import concourse.mybir as mybir
+from concourse.masks import make_identity
+
+F32 = mybir.dt.float32
+BF16 = mybir.dt.bfloat16
+U32 = mybir.dt.uint32
+U8 = mybir.dt.uint8
+FP8X4 = mybir.dt.float8_e4m3fn_x4
+ACT = mybir.ActivationFunctionType
+ALU = mybir.AluOpType
+
+P = 128
+TOKENS = 8 * 512
+DIM = 1024
+HID = 512
+RANK = 128
+PACK = 4
+K_PASS = P * PACK
+PASSES = DIM // K_PASS
+N_TILES = TOKENS // P
+ROUND = 2
+N_ROUNDS = N_TILES // ROUND
+X_LOAD = 4
+XA_LOAD = 8
+FLIPS = 4
+LEAD = 6
+
+FLOPS = 2 * TOKENS * DIM * HID * 2 + 2 * TOKENS * RANK * HID * 2
+
+
+def tile_feedforward_pa_t_kernel(
+    tc, x, w1, w3, xa_up, b_up, xa_gate, b_gate, tw_up, tw_gate, out
+):
+    nc = tc.nc
+
+    x_view = x.flatten_outer_dims().rearrange("(p j) k -> p j k", j=N_TILES)
+    xa_up_view = xa_up.flatten_outer_dims().rearrange("(p j) r -> p j r", j=N_TILES)
+    xa_gate_view = xa_gate.flatten_outer_dims().rearrange("(p j) r -> p j r", j=N_TILES)
+    out_view = out.flatten_outer_dims().rearrange("(p j) h -> p j h", j=N_TILES)
+    tw_up_view = tw_up.rearrange("b (q j) -> (b q) j", j=N_TILES)
+    tw_gate_view = tw_gate.rearrange("b (q j) -> (b q) j", j=N_TILES)
+
+    with ExitStack() as ctx:
+        keep = ctx.enter_context(tc.tile_pool(name="keep", bufs=1))
+        w_stage = ctx.enter_context(tc.tile_pool(name="w_stage", bufs=2))
+        x_stage = ctx.enter_context(tc.tile_pool(name="x_stage", bufs=3))
+        sums = ctx.enter_context(tc.tile_pool(name="sums", bufs=LEAD + 4))
+        psum_mx = ctx.enter_context(tc.psum_pool(name="psum_mx", bufs=4))
+        psum_lora = ctx.enter_context(tc.psum_pool(name="psum_lora", bufs=2))
+        psum_flip = ctx.enter_context(tc.psum_pool(name="psum_flip", bufs=2))
+        ctx.enter_context(tc.manual_schedule())
+
+        tw_up_bf = keep.tile([P, N_TILES], BF16)
+        tw_gate_bf = keep.tile([P, N_TILES], BF16)
+        b_up_sb = keep.tile([RANK, HID], BF16)
+        b_gate_sb = keep.tile([RANK, HID], BF16)
+        nc.sync.dma_start(out=tw_up_bf[:], in_=tw_up_view)
+        nc.sync.dma_start(out=tw_gate_bf[:], in_=tw_gate_view)
+        nc.sync.dma_start(out=b_up_sb[:], in_=b_up)
+        nc.sync.dma_start(out=b_gate_sb[:], in_=b_gate)
+
+        xa_up_sb = keep.tile([P, N_TILES, RANK], BF16)
+        xa_gate_sb = keep.tile([P, N_TILES, RANK], BF16)
+        for first in range(0, N_TILES, XA_LOAD):
+            tiles = slice(first, first + XA_LOAD)
+            nc.sync.dma_start(out=xa_up_sb[:, tiles, :], in_=xa_up_view[:, tiles, :])
+            nc.sync.dma_start(out=xa_gate_sb[:, tiles, :], in_=xa_gate_view[:, tiles, :])
+
+        w1_raw = keep.tile([P, PASSES * PACK, HID], BF16)
+        w3_raw = keep.tile([P, PASSES * PACK, HID], BF16)
+        for raw, w in ((w1_raw, w1), (w3_raw, w3)):
+            nc.sync.dma_start(
+                out=raw[:].rearrange("p (q e) c -> p q (e c)", e=2),
+                in_=w.rearrange("(q p e) c -> p q (e c)", p=P, e=2),
+            )
+
+        x_raw = []
+        for first in range(0, N_TILES, X_LOAD):
+            x_part = keep.tile([P, X_LOAD, DIM], BF16, name="x_part%d" % first)
+            nc.sync.dma_start(out=x_part[:], in_=x_view[:, first : first + X_LOAD, :])
+            x_raw.append(x_part)
+
+        ident_bf = keep.tile([P, P], BF16)
+        ident_f32 = keep.tile([P, P], F32)
+        make_identity(nc, ident_bf[:])
+        make_identity(nc, ident_f32[:])
+
+        zero = keep.tile([P, 1], F32)
+        warm = keep.tile([P, 1], F32)
+        nc.vector.memset(zero[:], 0.0)
+        nc.scalar.activation(out=warm[:], in_=zero[:], func=ACT.Silu)
+
+        tw4_up = keep.tile([P, N_TILES], F32)
+        tw4_gate = keep.tile([P, N_TILES], F32)
+        nc.vector.tensor_scalar(tw4_up[:], tw_up_bf[:], 4.0, None, op0=ALU.mult)
+        nc.vector.tensor_scalar(tw4_gate[:], tw_gate_bf[:], 4.0, None, op0=ALU.mult)
+
+        xaT_up = keep.tile([RANK, N_TILES, P], BF16)
+        xaT_gate = keep.tile([RANK, N_TILES, P], BF16)
+
+        def flip_adapter_inputs(first):
+            for start in range(first, first + XA_LOAD, FLIPS):
+                up_bank = psum_mx.tile([RANK, FLIPS, P], BF16, tag="mx")
+                for i in range(FLIPS):
+                    nc.tensor.transpose(up_bank[:, i, :], xa_up_sb[:, start + i, :], ident_bf[:])
+                nc.vector.tensor_copy(out=xaT_up[:, start : start + FLIPS, :], in_=up_bank[:])
+                gate_bank = psum_mx.tile([RANK, FLIPS, P], BF16, tag="mx")
+                for i in range(FLIPS):
+                    nc.tensor.transpose(gate_bank[:, i, :], xa_gate_sb[:, start + i, :], ident_bf[:])
+                nc.scalar.copy(out=xaT_gate[:, start : start + FLIPS, :], in_=gate_bank[:])
+
+        gate_sum = {}
+        up_sum = {}
+
+        def adapters(j):
+            r, a = divmod(j, ROUND)
+            gate_lora = psum_lora.tile([P, HID], F32, tag="lora")
+            nc.tensor.matmul(gate_lora[:], lhsT=xaT_gate[:, j, :], rhs=b_gate_sb[:], start=True, stop=True)
+            gate_sum[j] = sums.tile([P, HID], F32, name="gate_sum%d" % j, tag="gate_sum")
+            nc.scalar.activation(
+                out=gate_sum[j][:], in_=gate_lora[:], func=ACT.Copy, scale=tw4_gate[:, j : j + 1]
+            )
+            up_lora = psum_lora.tile([P, HID], F32, tag="lora")
+            nc.tensor.matmul(up_lora[:], lhsT=xaT_up[:, j, :], rhs=b_up_sb[:], start=True, stop=True)
+            if a == 0:
+                up_sum[r] = sums.tile([P, ROUND, HID], F32, name="up_sum%d" % r, tag="up_sum")
+            nc.vector.tensor_scalar(
+                up_sum[r][:, a, :], up_lora[:], tw4_up[:, j : j + 1], None, op0=ALU.mult
+            )
+
+        def quantise_weight(raw, codes, scales):
+            grouped = []
+            for g in range(PASSES):
+                rows = raw[:, PACK * g : PACK * (g + 1), :]
+                side_by_side = w_stage.tile([P, HID, PACK], BF16, name="w_grouped%d" % g, align_bytes=64)
+                copy = nc.vector.tensor_copy if g == 0 else nc.scalar.copy
+                copy(
+                    out=side_by_side[:].rearrange("p (c i) t -> p c t i", i=4),
+                    in_=rows.rearrange("p t (c i) -> p c t i", i=4),
+                )
+                grouped.append(side_by_side)
+            for g in range(PASSES):
+                nc.vector.quantize_mx(
+                    out=codes[:, g, :].bitcast(FP8X4),
+                    scales=scales[:, g, :],
+                    in_=grouped[g][:].rearrange("p c t -> p (c t)"),
+                )
+
+        w1_codes = keep.tile([P, PASSES, HID], U32, align_bytes=64)
+        w1_scales = keep.tile([P, PASSES, HID], U8, align_bytes=64)
+        w3_codes = keep.tile([P, PASSES, HID], U32, align_bytes=64)
+        w3_scales = keep.tile([P, PASSES, HID], U8, align_bytes=64)
+
+        x_grouped = {}
+        x_codes = {}
+        x_scales = {}
+
+        def flip_x(r):
+            x_grouped[r] = x_stage.tile([P, ROUND * DIM], BF16, name="x_grouped%d" % r, tag="x_grouped", align_bytes=64)
+            for a in range(ROUND):
+                part, i = divmod(ROUND * r + a, X_LOAD)
+                words = x_raw[part][:, i, :].bitcast(F32)
+                bank = psum_flip.tile([P, FLIPS, P], F32, tag="flip")
+                for q in range(FLIPS):
+                    nc.tensor.transpose(bank[:, q, :], words[:, q * P : (q + 1) * P], ident_f32[:])
+                nc.scalar.copy(
+                    out=x_grouped[r][:, a * DIM : (a + 1) * DIM]
+                    .bitcast(F32)
+                    .rearrange("p (g r u) -> p g r u", g=PASSES, u=2),
+                    in_=bank[:].rearrange("p (g u) r -> p g r u", u=2),
+                )
+
+        def quantise_x(r):
+            x_codes[r] = x_stage.tile([P, ROUND, PASSES, P], U32, name="x_codes%d" % r, tag="x_codes", align_bytes=64)
+            x_scales[r] = x_stage.tile([P, ROUND, PASSES, P], U8, name="x_scales%d" % r, tag="x_scales", align_bytes=64)
+            nc.vector.quantize_mx(
+                out=x_codes[r][:].rearrange("p a g r -> p (a g r)").bitcast(FP8X4),
+                scales=x_scales[r][:].rearrange("p a g r -> p (a g r)"),
+                in_=x_grouped[r][:],
+            )
+
+        def project(j, codes, scales):
+            r, a = divmod(j, ROUND)
+            acc = psum_mx.tile([P, HID], F32, tag="mx")
+            for g in range(PASSES):
+                nc.tensor.matmul_mx(
+                    out=acc[:],
+                    lhsT=x_codes[r][:, a, g, :].bitcast(FP8X4),
+                    lhsT_scale=x_scales[r][:, a, g, :],
+                    rhs=codes[:, g, :].bitcast(FP8X4),
+                    rhs_scale=scales[:, g, :],
+                    start=(g == 0),
+                    stop=(g == PASSES - 1),
+                )
+            return acc
+
+        def finish(j):
+            r, a = divmod(j, ROUND)
+            gate_mx = project(j, w1_codes, w1_scales)
+            up_mx = project(j, w3_codes, w3_scales)
+            gate = gate_sum[j][:]
+            h = up_sum[r][:, a, :]
+            nc.vector.tensor_tensor(out=gate, in0=gate, in1=gate_mx[:], op=ALU.add)
+            nc.scalar.activation(out=gate, in_=gate, func=ACT.Silu)
+            nc.vector.tensor_tensor(out=h, in0=h, in1=up_mx[:], op=ALU.add)
+            nc.gpsimd.tensor_tensor(out=h, in0=h, in1=gate, op=ALU.mult)
+            if a == ROUND - 1:
+                nc.sync.dma_start(out=out_view[:, ROUND * r : ROUND * (r + 1), :], in_=up_sum[r][:])
+
+        flip_adapter_inputs(0)
+        for j in range(LEAD):
+            adapters(j)
+        for first in range(XA_LOAD, N_TILES, XA_LOAD):
+            flip_adapter_inputs(first)
+        quantise_weight(w1_raw, w1_codes, w1_scales)
+        quantise_weight(w3_raw, w3_codes, w3_scales)
+        flip_x(0)
+        quantise_x(0)
+        for r in range(N_ROUNDS):
+            if r + 1 < N_ROUNDS:
+                flip_x(r + 1)
+            for a in range(ROUND):
+                j = ROUND * r + a
+                if j + LEAD < N_TILES:
+                    adapters(j + LEAD)
+                finish(j)
+                if a == 0 and r + 1 < N_ROUNDS:
+                    quantise_x(r + 1)

@@ -25,7 +25,7 @@ N_ROUNDS = N_TILES // ROUND
 X_LOAD = 4
 XA_LOAD = 8
 FLIPS = 4
-LEAD = 6
+LEAD = 8
 
 FLOPS = 2 * TOKENS * DIM * HID * 2 + 2 * TOKENS * RANK * HID * 2
 
@@ -46,27 +46,31 @@ def tile_feedforward_pa_t_kernel(
         keep = ctx.enter_context(tc.tile_pool(name="keep", bufs=1))
         w_stage = ctx.enter_context(tc.tile_pool(name="w_stage", bufs=2))
         x_stage = ctx.enter_context(tc.tile_pool(name="x_stage", bufs=3))
-        sums = ctx.enter_context(tc.tile_pool(name="sums", bufs=LEAD + 4))
-        psum_mx = ctx.enter_context(tc.psum_pool(name="psum_mx", bufs=4))
-        psum_lora = ctx.enter_context(tc.psum_pool(name="psum_lora", bufs=2))
+        sums = ctx.enter_context(tc.tile_pool(name="sums", bufs=LEAD + 6))
+        psum_ring = ctx.enter_context(tc.psum_pool(name="psum_ring", bufs=6))
         psum_flip = ctx.enter_context(tc.psum_pool(name="psum_flip", bufs=2))
         ctx.enter_context(tc.manual_schedule())
+
+        xa_up_sb = keep.tile([P, N_TILES, RANK], BF16)
+        xa_gate_sb = keep.tile([P, N_TILES, RANK], BF16)
+
+        def load_adapter_inputs(first):
+            tiles = slice(first, first + XA_LOAD)
+            nc.sync.dma_start(out=xa_up_sb[:, tiles, :], in_=xa_up_view[:, tiles, :])
+            nc.sync.dma_start(out=xa_gate_sb[:, tiles, :], in_=xa_gate_view[:, tiles, :])
+
+        load_adapter_inputs(0)
 
         tw_up_bf = keep.tile([P, N_TILES], BF16)
         tw_gate_bf = keep.tile([P, N_TILES], BF16)
         b_up_sb = keep.tile([RANK, HID], BF16)
         b_gate_sb = keep.tile([RANK, HID], BF16)
-        nc.sync.dma_start(out=tw_up_bf[:], in_=tw_up_view)
-        nc.sync.dma_start(out=tw_gate_bf[:], in_=tw_gate_view)
-        nc.sync.dma_start(out=b_up_sb[:], in_=b_up)
         nc.sync.dma_start(out=b_gate_sb[:], in_=b_gate)
+        nc.sync.dma_start(out=b_up_sb[:], in_=b_up)
+        nc.sync.dma_start(out=tw_gate_bf[:], in_=tw_gate_view)
+        nc.sync.dma_start(out=tw_up_bf[:], in_=tw_up_view)
 
-        xa_up_sb = keep.tile([P, N_TILES, RANK], BF16)
-        xa_gate_sb = keep.tile([P, N_TILES, RANK], BF16)
-        for first in range(0, N_TILES, XA_LOAD):
-            tiles = slice(first, first + XA_LOAD)
-            nc.sync.dma_start(out=xa_up_sb[:, tiles, :], in_=xa_up_view[:, tiles, :])
-            nc.sync.dma_start(out=xa_gate_sb[:, tiles, :], in_=xa_gate_view[:, tiles, :])
+        load_adapter_inputs(XA_LOAD)
 
         w1_raw = keep.tile([P, PASSES * PACK, HID], BF16)
         w3_raw = keep.tile([P, PASSES * PACK, HID], BF16)
@@ -81,6 +85,9 @@ def tile_feedforward_pa_t_kernel(
             x_part = keep.tile([P, X_LOAD, DIM], BF16, name="x_part%d" % first)
             nc.sync.dma_start(out=x_part[:], in_=x_view[:, first : first + X_LOAD, :])
             x_raw.append(x_part)
+            if first == 0:
+                load_adapter_inputs(2 * XA_LOAD)
+                load_adapter_inputs(3 * XA_LOAD)
 
         ident_bf = keep.tile([P, P], BF16)
         ident_f32 = keep.tile([P, P], F32)
@@ -102,11 +109,11 @@ def tile_feedforward_pa_t_kernel(
 
         def flip_adapter_inputs(first):
             for start in range(first, first + XA_LOAD, FLIPS):
-                up_bank = psum_mx.tile([RANK, FLIPS, P], BF16, tag="mx")
+                up_bank = psum_ring.tile([RANK, FLIPS, P], BF16, tag="ring")
                 for i in range(FLIPS):
                     nc.tensor.transpose(up_bank[:, i, :], xa_up_sb[:, start + i, :], ident_bf[:])
                 nc.vector.tensor_copy(out=xaT_up[:, start : start + FLIPS, :], in_=up_bank[:])
-                gate_bank = psum_mx.tile([RANK, FLIPS, P], BF16, tag="mx")
+                gate_bank = psum_ring.tile([RANK, FLIPS, P], BF16, tag="ring")
                 for i in range(FLIPS):
                     nc.tensor.transpose(gate_bank[:, i, :], xa_gate_sb[:, start + i, :], ident_bf[:])
                 nc.scalar.copy(out=xaT_gate[:, start : start + FLIPS, :], in_=gate_bank[:])
@@ -115,19 +122,17 @@ def tile_feedforward_pa_t_kernel(
         up_sum = {}
 
         def adapters(j):
-            r, a = divmod(j, ROUND)
-            gate_lora = psum_lora.tile([P, HID], F32, tag="lora")
+            gate_lora = psum_ring.tile([P, HID], F32, tag="ring")
             nc.tensor.matmul(gate_lora[:], lhsT=xaT_gate[:, j, :], rhs=b_gate_sb[:], start=True, stop=True)
             gate_sum[j] = sums.tile([P, HID], F32, name="gate_sum%d" % j, tag="gate_sum")
             nc.scalar.activation(
                 out=gate_sum[j][:], in_=gate_lora[:], func=ACT.Copy, scale=tw4_gate[:, j : j + 1]
             )
-            up_lora = psum_lora.tile([P, HID], F32, tag="lora")
+            up_lora = psum_ring.tile([P, HID], F32, tag="ring")
             nc.tensor.matmul(up_lora[:], lhsT=xaT_up[:, j, :], rhs=b_up_sb[:], start=True, stop=True)
-            if a == 0:
-                up_sum[r] = sums.tile([P, ROUND, HID], F32, name="up_sum%d" % r, tag="up_sum")
+            up_sum[j] = sums.tile([P, HID], F32, name="up_sum%d" % j, tag="up_sum")
             nc.vector.tensor_scalar(
-                up_sum[r][:, a, :], up_lora[:], tw4_up[:, j : j + 1], None, op0=ALU.mult
+                up_sum[j][:], up_lora[:], tw4_up[:, j : j + 1], None, op0=ALU.mult
             )
 
         def quantise_weight(raw, codes, scales):
@@ -183,7 +188,7 @@ def tile_feedforward_pa_t_kernel(
 
         def project(j, codes, scales):
             r, a = divmod(j, ROUND)
-            acc = psum_mx.tile([P, HID], F32, tag="mx")
+            acc = psum_ring.tile([P, HID], F32, tag="ring")
             for g in range(PASSES):
                 nc.tensor.matmul_mx(
                     out=acc[:],
@@ -197,27 +202,32 @@ def tile_feedforward_pa_t_kernel(
             return acc
 
         def finish(j):
-            r, a = divmod(j, ROUND)
             gate_mx = project(j, w1_codes, w1_scales)
             up_mx = project(j, w3_codes, w3_scales)
             gate = gate_sum[j][:]
-            h = up_sum[r][:, a, :]
+            h = up_sum[j][:]
             nc.vector.tensor_tensor(out=gate, in0=gate, in1=gate_mx[:], op=ALU.add)
             nc.scalar.activation(out=gate, in_=gate, func=ACT.Silu)
             nc.vector.tensor_tensor(out=h, in0=h, in1=up_mx[:], op=ALU.add)
             nc.gpsimd.tensor_tensor(out=h, in0=h, in1=gate, op=ALU.mult)
-            if a == ROUND - 1:
-                nc.sync.dma_start(out=out_view[:, ROUND * r : ROUND * (r + 1), :], in_=up_sum[r][:])
+            nc.sync.dma_start(out=out_view[:, j, :], in_=h)
 
         flip_adapter_inputs(0)
-        for j in range(LEAD):
+        for j in range(0, 2):
             adapters(j)
-        for first in range(XA_LOAD, N_TILES, XA_LOAD):
-            flip_adapter_inputs(first)
+        flip_adapter_inputs(XA_LOAD)
+        for j in range(2, 4):
+            adapters(j)
         quantise_weight(w1_raw, w1_codes, w1_scales)
+        for j in range(4, 6):
+            adapters(j)
         quantise_weight(w3_raw, w3_codes, w3_scales)
+        for j in range(6, LEAD):
+            adapters(j)
         flip_x(0)
         quantise_x(0)
+        flip_adapter_inputs(2 * XA_LOAD)
+        flip_adapter_inputs(3 * XA_LOAD)
         for r in range(N_ROUNDS):
             if r + 1 < N_ROUNDS:
                 flip_x(r + 1)

@@ -135,17 +135,19 @@ def tile_feedforward_pa_t_kernel(
                 up_sum[j][:], up_lora[:], tw4_up[:, j : j + 1], None, op0=ALU.mult
             )
 
-        def quantise_weight(raw, codes, scales):
+        def regroup_weight(raw, copies):
             grouped = []
             for g in range(PASSES):
                 rows = raw[:, PACK * g : PACK * (g + 1), :]
                 side_by_side = w_stage.tile([P, HID, PACK], BF16, name="w_grouped%d" % g, align_bytes=64)
-                copy = nc.vector.tensor_copy if g == 0 else nc.scalar.copy
-                copy(
+                copies[g](
                     out=side_by_side[:].rearrange("p (c i) t -> p c t i", i=4),
                     in_=rows.rearrange("p t (c i) -> p c t i", i=4),
                 )
                 grouped.append(side_by_side)
+            return grouped
+
+        def quantise_weight(grouped, codes, scales):
             for g in range(PASSES):
                 nc.vector.quantize_mx(
                     out=codes[:, g, :].bitcast(FP8X4),
@@ -209,7 +211,8 @@ def tile_feedforward_pa_t_kernel(
             nc.vector.tensor_tensor(out=gate, in0=gate, in1=gate_mx[:], op=ALU.add)
             nc.scalar.activation(out=gate, in_=gate, func=ACT.Silu)
             nc.vector.tensor_tensor(out=h, in0=h, in1=up_mx[:], op=ALU.add)
-            nc.gpsimd.tensor_tensor(out=h, in0=h, in1=gate, op=ALU.mult)
+            multiplier = nc.vector if j == N_TILES - 1 else nc.gpsimd
+            multiplier.tensor_tensor(out=h, in0=h, in1=gate, op=ALU.mult)
             nc.sync.dma_start(out=out_view[:, j, :], in_=h)
 
         flip_adapter_inputs(0)
@@ -218,12 +221,14 @@ def tile_feedforward_pa_t_kernel(
         flip_adapter_inputs(XA_LOAD)
         for j in range(2, 4):
             adapters(j)
-        quantise_weight(w1_raw, w1_codes, w1_scales)
+        w1_grouped = regroup_weight(w1_raw, (nc.vector.tensor_copy, nc.vector.tensor_copy))
         for j in range(4, 6):
             adapters(j)
-        quantise_weight(w3_raw, w3_codes, w3_scales)
+        quantise_weight(w1_grouped, w1_codes, w1_scales)
+        w3_grouped = regroup_weight(w3_raw, (nc.vector.tensor_copy, nc.scalar.copy))
         for j in range(6, LEAD):
             adapters(j)
+        quantise_weight(w3_grouped, w3_codes, w3_scales)
         flip_x(0)
         quantise_x(0)
         flip_adapter_inputs(2 * XA_LOAD)

@@ -234,12 +234,14 @@ def tile_feedforward_pa_t_kernel(
         flip_adapter_inputs(2 * XA_LOAD)
         flip_adapter_inputs(3 * XA_LOAD)
         for r in range(N_ROUNDS):
+            j = ROUND * r
+            if j + LEAD < N_TILES:
+                adapters(j + LEAD)
             if r + 1 < N_ROUNDS:
                 flip_x(r + 1)
-            for a in range(ROUND):
-                j = ROUND * r + a
-                if j + LEAD < N_TILES:
-                    adapters(j + LEAD)
-                finish(j)
-                if a == 0 and r + 1 < N_ROUNDS:
-                    quantise_x(r + 1)
+            if j + LEAD < N_TILES:
+                adapters(j + LEAD + 1)
+            finish(j)
+            if r + 1 < N_ROUNDS:
+                quantise_x(r + 1)
+            finish(j + 1)

from contextlib import ExitStack

import concourse.mybir as mybir
from concourse.masks import make_identity

F32 = mybir.dt.float32
BF16 = mybir.dt.bfloat16
U32 = mybir.dt.uint32
U8 = mybir.dt.uint8
FP8X4 = mybir.dt.float8_e4m3fn_x4
ACT = mybir.ActivationFunctionType
ALU = mybir.AluOpType

P = 128
TOKENS = 8 * 512
DIM = 1024
HID = 512
RANK = 128
PACK = 4
K_PASS = P * PACK
PASSES = DIM // K_PASS
N_TILES = TOKENS // P
ROUND = 2
N_ROUNDS = N_TILES // ROUND
X_LOAD = 4
XA_LOAD = 8
FLIPS = 4
LEAD = 8

FLOPS = 2 * TOKENS * DIM * HID * 2 + 2 * TOKENS * RANK * HID * 2


def tile_feedforward_pa_t_kernel(
    tc, x, w1, w3, xa_up, b_up, xa_gate, b_gate, tw_up, tw_gate, out
):
    nc = tc.nc

    x_view = x.flatten_outer_dims().rearrange("(p j) k -> p j k", j=N_TILES)
    xa_up_view = xa_up.flatten_outer_dims().rearrange("(p j) r -> p j r", j=N_TILES)
    xa_gate_view = xa_gate.flatten_outer_dims().rearrange("(p j) r -> p j r", j=N_TILES)
    out_view = out.flatten_outer_dims().rearrange("(p j) h -> p j h", j=N_TILES)
    tw_up_view = tw_up.rearrange("b (q j) -> (b q) j", j=N_TILES)
    tw_gate_view = tw_gate.rearrange("b (q j) -> (b q) j", j=N_TILES)

    with ExitStack() as ctx:
        keep = ctx.enter_context(tc.tile_pool(name="keep", bufs=1))
        w_stage = ctx.enter_context(tc.tile_pool(name="w_stage", bufs=2))
        x_stage = ctx.enter_context(tc.tile_pool(name="x_stage", bufs=3))
        sums = ctx.enter_context(tc.tile_pool(name="sums", bufs=LEAD + 6))
        psum_ring = ctx.enter_context(tc.psum_pool(name="psum_ring", bufs=6))
        psum_flip = ctx.enter_context(tc.psum_pool(name="psum_flip", bufs=2))
        ctx.enter_context(tc.manual_schedule())

        xa_up_sb = keep.tile([P, N_TILES, RANK], BF16)
        xa_gate_sb = keep.tile([P, N_TILES, RANK], BF16)

        def load_adapter_inputs(first):
            tiles = slice(first, first + XA_LOAD)
            nc.sync.dma_start(out=xa_up_sb[:, tiles, :], in_=xa_up_view[:, tiles, :])
            nc.sync.dma_start(out=xa_gate_sb[:, tiles, :], in_=xa_gate_view[:, tiles, :])

        load_adapter_inputs(0)

        tw_up_bf = keep.tile([P, N_TILES], BF16)
        tw_gate_bf = keep.tile([P, N_TILES], BF16)
        b_up_sb = keep.tile([RANK, HID], BF16)
        b_gate_sb = keep.tile([RANK, HID], BF16)
        nc.sync.dma_start(out=b_gate_sb[:], in_=b_gate)
        nc.sync.dma_start(out=b_up_sb[:], in_=b_up)
        nc.sync.dma_start(out=tw_gate_bf[:], in_=tw_gate_view)
        nc.sync.dma_start(out=tw_up_bf[:], in_=tw_up_view)

        load_adapter_inputs(XA_LOAD)

        w1_raw = keep.tile([P, PASSES * PACK, HID], BF16)
        w3_raw = keep.tile([P, PASSES * PACK, HID], BF16)
        for raw, w in ((w1_raw, w1), (w3_raw, w3)):
            nc.sync.dma_start(
                out=raw[:].rearrange("p (q e) c -> p q (e c)", e=2),
                in_=w.rearrange("(q p e) c -> p q (e c)", p=P, e=2),
            )

        x_raw = []
        for first in range(0, N_TILES, X_LOAD):
            x_part = keep.tile([P, X_LOAD, DIM], BF16, name="x_part%d" % first)
            nc.sync.dma_start(out=x_part[:], in_=x_view[:, first : first + X_LOAD, :])
            x_raw.append(x_part)
            if first == 0:
                load_adapter_inputs(2 * XA_LOAD)
                load_adapter_inputs(3 * XA_LOAD)

        ident_bf = keep.tile([P, P], BF16)
        ident_f32 = keep.tile([P, P], F32)
        make_identity(nc, ident_bf[:])
        make_identity(nc, ident_f32[:])

        zero = keep.tile([P, 1], F32)
        warm = keep.tile([P, 1], F32)
        nc.vector.memset(zero[:], 0.0)
        nc.scalar.activation(out=warm[:], in_=zero[:], func=ACT.Silu)

        tw4_up = keep.tile([P, N_TILES], F32)
        tw4_gate = keep.tile([P, N_TILES], F32)
        nc.vector.tensor_scalar(tw4_up[:], tw_up_bf[:], 4.0, None, op0=ALU.mult)
        nc.vector.tensor_scalar(tw4_gate[:], tw_gate_bf[:], 4.0, None, op0=ALU.mult)

        xaT_up = keep.tile([RANK, N_TILES, P], BF16)
        xaT_gate = keep.tile([RANK, N_TILES, P], BF16)

        def flip_adapter_inputs(first):
            for start in range(first, first + XA_LOAD, FLIPS):
                up_bank = psum_ring.tile([RANK, FLIPS, P], BF16, tag="ring")
                for i in range(FLIPS):
                    nc.tensor.transpose(up_bank[:, i, :], xa_up_sb[:, start + i, :], ident_bf[:])
                nc.vector.tensor_copy(out=xaT_up[:, start : start + FLIPS, :], in_=up_bank[:])
                gate_bank = psum_ring.tile([RANK, FLIPS, P], BF16, tag="ring")
                for i in range(FLIPS):
                    nc.tensor.transpose(gate_bank[:, i, :], xa_gate_sb[:, start + i, :], ident_bf[:])
                nc.scalar.copy(out=xaT_gate[:, start : start + FLIPS, :], in_=gate_bank[:])

        gate_sum = {}
        up_sum = {}

        def adapters(j):
            gate_lora = psum_ring.tile([P, HID], F32, tag="ring")
            nc.tensor.matmul(gate_lora[:], lhsT=xaT_gate[:, j, :], rhs=b_gate_sb[:], start=True, stop=True)
            gate_sum[j] = sums.tile([P, HID], F32, name="gate_sum%d" % j, tag="gate_sum")
            nc.scalar.activation(
                out=gate_sum[j][:], in_=gate_lora[:], func=ACT.Copy, scale=tw4_gate[:, j : j + 1]
            )
            up_lora = psum_ring.tile([P, HID], F32, tag="ring")
            nc.tensor.matmul(up_lora[:], lhsT=xaT_up[:, j, :], rhs=b_up_sb[:], start=True, stop=True)
            up_sum[j] = sums.tile([P, HID], F32, name="up_sum%d" % j, tag="up_sum")
            nc.vector.tensor_scalar(
                up_sum[j][:], up_lora[:], tw4_up[:, j : j + 1], None, op0=ALU.mult
            )

        def regroup_weight(raw, copies):
            grouped = []
            for g in range(PASSES):
                rows = raw[:, PACK * g : PACK * (g + 1), :]
                side_by_side = w_stage.tile([P, HID, PACK], BF16, name="w_grouped%d" % g, align_bytes=64)
                copies[g](
                    out=side_by_side[:].rearrange("p (c i) t -> p c t i", i=4),
                    in_=rows.rearrange("p t (c i) -> p c t i", i=4),
                )
                grouped.append(side_by_side)
            return grouped

        def quantise_weight(grouped, codes, scales):
            for g in range(PASSES):
                nc.vector.quantize_mx(
                    out=codes[:, g, :].bitcast(FP8X4),
                    scales=scales[:, g, :],
                    in_=grouped[g][:].rearrange("p c t -> p (c t)"),
                )

        w1_codes = keep.tile([P, PASSES, HID], U32, align_bytes=64)
        w1_scales = keep.tile([P, PASSES, HID], U8, align_bytes=64)
        w3_codes = keep.tile([P, PASSES, HID], U32, align_bytes=64)
        w3_scales = keep.tile([P, PASSES, HID], U8, align_bytes=64)

        x_grouped = {}
        x_codes = {}
        x_scales = {}

        def flip_x(r):
            x_grouped[r] = x_stage.tile([P, ROUND * DIM], BF16, name="x_grouped%d" % r, tag="x_grouped", align_bytes=64)
            for a in range(ROUND):
                part, i = divmod(ROUND * r + a, X_LOAD)
                words = x_raw[part][:, i, :].bitcast(F32)
                bank = psum_flip.tile([P, FLIPS, P], F32, tag="flip")
                for q in range(FLIPS):
                    nc.tensor.transpose(bank[:, q, :], words[:, q * P : (q + 1) * P], ident_f32[:])
                nc.scalar.copy(
                    out=x_grouped[r][:, a * DIM : (a + 1) * DIM]
                    .bitcast(F32)
                    .rearrange("p (g r u) -> p g r u", g=PASSES, u=2),
                    in_=bank[:].rearrange("p (g u) r -> p g r u", u=2),
                )

        def quantise_x(r):
            x_codes[r] = x_stage.tile([P, ROUND, PASSES, P], U32, name="x_codes%d" % r, tag="x_codes", align_bytes=64)
            x_scales[r] = x_stage.tile([P, ROUND, PASSES, P], U8, name="x_scales%d" % r, tag="x_scales", align_bytes=64)
            nc.vector.quantize_mx(
                out=x_codes[r][:].rearrange("p a g r -> p (a g r)").bitcast(FP8X4),
                scales=x_scales[r][:].rearrange("p a g r -> p (a g r)"),
                in_=x_grouped[r][:],
            )

        def project(j, codes, scales):
            r, a = divmod(j, ROUND)
            acc = psum_ring.tile([P, HID], F32, tag="ring")
            for g in range(PASSES):
                nc.tensor.matmul_mx(
                    out=acc[:],
                    lhsT=x_codes[r][:, a, g, :].bitcast(FP8X4),
                    lhsT_scale=x_scales[r][:, a, g, :],
                    rhs=codes[:, g, :].bitcast(FP8X4),
                    rhs_scale=scales[:, g, :],
                    start=(g == 0),
                    stop=(g == PASSES - 1),
                )
            return acc

        def finish(j):
            gate_mx = project(j, w1_codes, w1_scales)
            up_mx = project(j, w3_codes, w3_scales)
            gate = gate_sum[j][:]
            h = up_sum[j][:]
            nc.vector.tensor_tensor(out=gate, in0=gate, in1=gate_mx[:], op=ALU.add)
            nc.scalar.activation(out=gate, in_=gate, func=ACT.Silu)
            nc.vector.tensor_tensor(out=h, in0=h, in1=up_mx[:], op=ALU.add)
            multiplier = nc.vector if j == N_TILES - 1 else nc.gpsimd
            multiplier.tensor_tensor(out=h, in0=h, in1=gate, op=ALU.mult)
            nc.sync.dma_start(out=out_view[:, j, :], in_=h)

        flip_adapter_inputs(0)
        for j in range(0, 2):
            adapters(j)
        flip_adapter_inputs(XA_LOAD)
        for j in range(2, 4):
            adapters(j)
        w1_grouped = regroup_weight(w1_raw, (nc.vector.tensor_copy, nc.vector.tensor_copy))
        for j in range(4, 6):
            adapters(j)
        quantise_weight(w1_grouped, w1_codes, w1_scales)
        w3_grouped = regroup_weight(w3_raw, (nc.vector.tensor_copy, nc.scalar.copy))
        for j in range(6, LEAD):
            adapters(j)
        quantise_weight(w3_grouped, w3_codes, w3_scales)
        flip_x(0)
        quantise_x(0)
        flip_adapter_inputs(2 * XA_LOAD)
        flip_adapter_inputs(3 * XA_LOAD)
        for r in range(N_ROUNDS):
            j = ROUND * r
            if j + LEAD < N_TILES:
                adapters(j + LEAD)
            if r + 1 < N_ROUNDS:
                flip_x(r + 1)
            if j + LEAD < N_TILES:
                adapters(j + LEAD + 1)
            finish(j)
            if r + 1 < N_ROUNDS:
                quantise_x(r + 1)
            finish(j + 1)
